import numpy as np
import ml_dtypes


def mxq(x, axis, fmt="e4m3"):
    dtype, down = {"e4m3": (ml_dtypes.float8_e4m3fn, 7), "e5m2": (ml_dtypes.float8_e5m2, 14)}[fmt]
    v = np.moveaxis(np.asarray(x, np.float32).astype(ml_dtypes.bfloat16).astype(np.float64), axis, -1)
    blocks = v.reshape(v.shape[:-1] + (-1, 32))
    amax = np.abs(blocks).max(-1, keepdims=True)
    byte = np.maximum(np.where(amax > 0, np.frexp(amax)[1] - 1 + 127, 0) - down, 1)
    scale = np.exp2(byte - 127.0)
    codes = (blocks / scale).astype(np.float32).astype(dtype).astype(np.float64)
    return np.moveaxis((codes * scale).reshape(v.shape), -1, axis)


WIDE = False


def mx_kscale(k):
    if not WIDE:
        return np.ones(k)
    levels = np.array([10, -10, 5, -5, 0])
    a = np.random.permutation(np.resize(levels, k // 512 * 4)).reshape(k // 512, 4)
    idx = np.arange(k)
    return np.exp2(a[idx // 512, idx % 128 // 32])


BF16 = ml_dtypes.bfloat16


def bf(x):
    return np.asarray(x, np.float32).astype(BF16)


def f64(x):
    return np.asarray(x).astype(np.float64)


E2M1 = np.array([0.0, 0.5, 1.0, 1.5, 2.0, 3.0, 4.0, 6.0, -0.0, -0.5, -1.0, -1.5, -2.0, -3.0, -4.0, -6.0])


def pack_weight(w, fmt):
    k, n = w.shape
    w = f64(bf(w)).reshape(k // 32, 32, n)
    amax = np.abs(w).max(1)
    if fmt == "e4m3":
        byte = np.frexp(amax)[1] - 1 + 127 - 7
    else:
        mant, ex = np.frexp(amax / 6.0)
        byte = np.where(mant > 0.5, ex, ex - 1) + 127
    byte = np.clip(np.where(amax > 0, byte, 1), 1, 254)
    scaled = (w * np.exp2(127.0 - byte)[:, None, :]).reshape(k, n).astype(np.float32)
    by_word = np.ascontiguousarray(scaled.reshape(k // 512, 128, 4, n).transpose(0, 1, 3, 2))
    if fmt == "e4m3":
        words = by_word.astype(ml_dtypes.float8_e4m3fn).view(np.uint8)
    else:
        c = by_word.astype(ml_dtypes.float4_e2m1fn).view(np.uint8) & 0xF
        words = c[..., 0::2] | (c[..., 1::2] << 4)
    return np.ascontiguousarray(words), np.ascontiguousarray(byte.astype(np.uint8).reshape(k // 512, 16, n))


def unpack_weight(words, scales, fmt):
    g, p, n, _ = words.shape
    if fmt == "e4m3":
        vals = np.ascontiguousarray(words).view(ml_dtypes.float8_e4m3fn).astype(np.float64)
    else:
        nib = np.empty((g, p, n, 4), np.uint8)
        nib[..., 0::2] = words & 0xF
        nib[..., 1::2] = words >> 4
        vals = E2M1[nib]
    vals = vals * np.repeat(np.exp2(scales.astype(np.float64) - 127.0), 8, axis=1)[..., None]
    return vals.transpose(0, 1, 3, 2).reshape(g * 512, n)


T, B, D, U, V, E = 4, 256, 512, 512, 512, 8
G = 2 * E


def softmax(v):
    e = np.exp(v - v.max(-1, keepdims=True))
    return e / e.sum(-1, keepdims=True)


def setup_inputs():
    rn = np.random.standard_normal
    s = mx_kscale(U)
    task_h = bf(np.abs(rn((T, B, U))) * 0.55 * s)
    share_h = bf(np.abs(rn((B, U))) * 0.5 * s)
    ews1 = rn((U, V, E)) * 2.0 / np.sqrt(U) / s[:, None, None]
    ews1_words, ews1_scales = pack_weight(ews1.reshape(U, V * E), "e4m3")
    ebs1 = bf(rn((V, E)) * 0.5)
    ew1 = rn((T, U, V, E)) * 2.0 / np.sqrt(U) / s[None, :, None, None]
    ew1_words, ew1_scales = pack_weight(ew1.reshape(T, U, V * E).reshape(-1, V * E), "e4m3")
    eb1 = bf(rn((T, V, E)) * 0.5)
    gate_pre1 = bf(rn((T, B, G)))
    gb1 = bf(rn((T, G)) * 0.5)
    return {
        "task_h": task_h,
        "share_h": share_h,
        "ews1_words": ews1_words,
        "ews1_scales": ews1_scales,
        "ebs1": ebs1,
        "ew1_words": ew1_words,
        "ew1_scales": ew1_scales,
        "eb1": eb1,
        "gate_pre1": gate_pre1,
        "gb1": gb1,
    }


def reference(task_h, share_h, ews1_words, ews1_scales, ebs1, ew1_words, ew1_scales, eb1, gate_pre1, gb1):
    es = np.maximum((mxq(f64(share_h), 1, "e4m3") @ unpack_weight(ews1_words, ews1_scales, "e4m3")).reshape(B, V, E) + f64(ebs1), 0.0)
    et = np.maximum((mxq(f64(task_h), 2, "e4m3") @ unpack_weight(ew1_words, ew1_scales, "e4m3").reshape(T, U, V * E)).reshape(T, B, V, E) + f64(eb1)[:, None], 0.0)
    g = softmax(f64(gate_pre1) + f64(gb1)[:, None])
    comb = np.concatenate([et, np.broadcast_to(es, et.shape)], axis=-1)
    return (comb * g[:, :, None, :]).sum(-1)

@@ -1,0 +1,227 @@
+from contextlib import ExitStack
+
+import concourse.mybir as mybir
+from concourse.masks import make_identity
+
+F32 = mybir.dt.float32
+BF16 = mybir.dt.bfloat16
+I32 = mybir.dt.int32
+U32 = mybir.dt.uint32
+U8 = mybir.dt.uint8
+FP8X4 = mybir.dt.float8_e4m3fn_x4
+ALU = mybir.AluOpType
+ACT = mybir.ActivationFunctionType
+AX = mybir.AxisListType
+
+P = 128
+TASKS = 4
+STREAMS = TASKS + 1
+SHARED = TASKS
+ROWS = 256
+ROW_TILES = ROWS // P
+FEATURES = 512
+UNITS = 512
+EXPERTS = 8
+COLS = UNITS * EXPERTS
+COL_TILES = COLS // P
+GATES = 2 * EXPERTS
+CHUNK_TILES = 4
+CHUNK_COLS = CHUNK_TILES * P
+CHUNK_UNITS = CHUNK_COLS // EXPERTS
+CHUNKS = COLS // CHUNK_COLS
+GROUPS = CHUNKS * ROW_TILES
+QUARTER = COLS // 4
+
+FLOPS = 2 * STREAMS * ROWS * FEATURES * COLS
+
+
+def tile_plelayer_pb_e_kernel(
+    tc, task_h, share_h, ews1_words, ews1_scales, ebs1, ew1_words, ew1_scales, eb1, gate_pre1, gb1, out
+):
+    nc = tc.nc
+    with ExitStack() as stack:
+        stack.enter_context(tc.manual_schedule())
+        keep = stack.enter_context(tc.tile_pool(name="keep", bufs=1))
+        y_pool = stack.enter_context(tc.tile_pool(name="y", bufs=2))
+        acc_pool = stack.enter_context(tc.tile_pool(name="acc", bufs=4))
+        z_pool = stack.enter_context(tc.psum_pool(name="z", bufs=2))
+        yt_pool = stack.enter_context(tc.psum_pool(name="yt", bufs=6))
+
+        identity = keep.tile([P, P], F32)
+        make_identity(nc, identity[:])
+
+        bias_rows = keep.tile([P, 2, P], BF16)
+        nc.vector.memset(bias_rows[:, 1, :], 0.0)
+        nc.scalar.dma_start(
+            out=bias_rows[:, 0, :], in_=eb1.rearrange("t v e -> (t v e)").rearrange("(r c) -> r c", c=P)
+        )
+        nc.scalar.dma_start(
+            out=bias_rows[0:COL_TILES, 1, :], in_=ebs1.rearrange("v e -> (v e)").rearrange("(r c) -> r c", c=P)
+        )
+        gate_pre = keep.tile([P, TASKS * ROW_TILES, GATES], BF16)
+        nc.scalar.dma_start(out=gate_pre[:], in_=gate_pre1.rearrange("t (h p) g -> p (t h) g", p=P))
+        gate_bias = keep.tile([P, TASKS, GATES], BF16)
+        nc.scalar.dma_start(
+            out=gate_bias[:].rearrange("p t g -> p (t g)"), in_=gb1.rearrange("t g -> (t g)").partition_broadcast(P)
+        )
+
+        x_rows = keep.tile([P, STREAMS, ROW_TILES, FEATURES], BF16)
+        for t in range(TASKS):
+            nc.sync.dma_start(out=x_rows[:, t, :, :], in_=task_h[t].rearrange("(h p) u -> p h u", p=P))
+        nc.sync.dma_start(out=x_rows[:, SHARED, :, :], in_=share_h.rearrange("(h p) u -> p h u", p=P))
+
+        task_planes = keep.tile([P, COLS], U8, align_bytes=64)
+        shared_planes = keep.tile([P, QUARTER], U8, align_bytes=64)
+        nc.vector.memset(task_planes[:].bitcast(I32), 0)
+        nc.vector.memset(shared_planes[:].bitcast(I32), 0)
+        for quad in range(4):
+            nc.sync.dma_start(
+                out=task_planes[32 * quad : 32 * quad + 16, :].bitcast(I32),
+                in_=ew1_scales[:, 4 * quad : 4 * quad + 4, :].bitcast(I32),
+            )
+        for quad in range(4):
+            nc.sync.dma_start(
+                out=shared_planes[32 * quad : 32 * quad + 16, :].bitcast(I32),
+                in_=ews1_scales[0, 4 * quad : 4 * quad + 4, :].bitcast(I32).rearrange("r (k n) -> k r n", k=4),
+            )
+
+        words = keep.tile([P, STREAMS, COLS], U32, align_bytes=64)
+        task_words = ew1_words.rearrange("t p n k -> t p (n k)").bitcast(I32)
+        shared_words = ews1_words.rearrange("g p n k -> g p (n k)").bitcast(I32)
+        for c in range(CHUNKS):
+            cols = slice(c * CHUNK_COLS, (c + 1) * CHUNK_COLS)
+            nc.sync.dma_start(
+                out=words[:, 0:TASKS, cols].bitcast(I32), in_=task_words[:, :, cols].rearrange("t p n -> p t n")
+            )
+            nc.sync.dma_start(out=words[:, SHARED, cols].bitcast(I32), in_=shared_words[0, :, cols])
+
+        bias_rows_f = keep.tile([P, 2, P], F32)
+        nc.vector.tensor_copy(out=bias_rows_f[:], in_=bias_rows[:])
+        bias_t = z_pool.tile([P, 2, P], F32, tag="z")
+        for plane in range(2):
+            nc.tensor.transpose(out=bias_t[:, plane, :], in_=bias_rows_f[:, plane, :], identity=identity[:])
+        bias_cols = keep.tile([P, 2, P], F32)
+        nc.vector.tensor_copy(out=bias_cols[:], in_=bias_t[:])
+
+        pairs = TASKS * ROW_TILES
+        logits = keep.tile([P, pairs, GATES], F32)
+        nc.vector.tensor_tensor(
+            out=logits[:].rearrange("p (t h) g -> p t h g", h=ROW_TILES),
+            in0=gate_pre[:].rearrange("p (t h) g -> p t h g", h=ROW_TILES),
+            in1=gate_bias[:].unsqueeze(2).to_broadcast([P, TASKS, ROW_TILES, GATES]),
+            op=ALU.add,
+        )
+        top = keep.tile([P, pairs], F32)
+        nc.vector.tensor_reduce(out=top[:], in_=logits[:], axis=AX.X, op=ALU.max)
+        shifted = keep.tile([P, pairs, GATES], F32)
+        nc.vector.tensor_tensor(
+            out=shifted[:], in0=logits[:], in1=top[:].unsqueeze(2).to_broadcast([P, pairs, GATES]), op=ALU.subtract
+        )
+        powers = keep.tile([P, pairs, GATES], F32)
+        nc.scalar.activation(out=powers[:], in_=shifted[:], func=ACT.Exp)
+
+        grouped = keep.tile([P, STREAMS, ROWS * 4], BF16, align_bytes=64)
+        x_codes = keep.tile([P, STREAMS, ROWS], U32, align_bytes=64)
+        x_planes = keep.tile([P, STREAMS, ROWS], U8, align_bytes=64)
+        for s in range(STREAMS):
+            x_t = z_pool.tile([P, 2, ROWS], F32, tag="z")
+            for h in range(ROW_TILES):
+                x_words = x_rows[:, s, h, :].bitcast(F32)
+                for half in range(2):
+                    nc.tensor.transpose(
+                        out=x_t[:, half, h * P : (h + 1) * P],
+                        in_=x_words[:, half : FEATURES // 2 : 2],
+                        identity=identity[:],
+                    )
+            side_by_side = grouped[:, s, :].bitcast(F32).rearrange("p (b half) -> p b half", half=2)
+            if s % 2 == 0:
+                nc.vector.tensor_copy(out=side_by_side, in_=x_t[:].rearrange("p half b -> p b half"))
+            else:
+                nc.scalar.copy(out=side_by_side, in_=x_t[:].rearrange("p half b -> p b half"))
+            for ready in [s - 2] if s < STREAMS - 1 else [s - 2, s - 1, s]:
+                if ready >= 0:
+                    nc.vector.quantize_mx(
+                        out=x_codes[:, ready, :].bitcast(FP8X4),
+                        scales=x_planes[:, ready, :],
+                        in_=grouped[:, ready, :],
+                    )
+
+        total = keep.tile([P, pairs], F32)
+        nc.vector.tensor_reduce(out=total[:], in_=powers[:], axis=AX.X, op=ALU.add)
+        inverse = keep.tile([P, pairs], F32)
+        nc.vector.reciprocal(out=inverse[:], in_=total[:])
+        gate = keep.tile([P, pairs, GATES], F32)
+        nc.vector.tensor_tensor(
+            out=gate[:], in0=powers[:], in1=inverse[:].unsqueeze(2).to_broadcast([P, pairs, GATES]), op=ALU.mult
+        )
+
+        def experts(c, streams, y, vector_helps):
+            for s in streams:
+                for first in range(0, CHUNK_TILES, 2):
+                    z = z_pool.tile([P, 2, ROWS], F32, tag="z")
+                    for i in range(2):
+                        j = c * CHUNK_TILES + first + i
+                        cols = slice(j * P, (j + 1) * P)
+                        if s == SHARED:
+                            k = j * P // QUARTER
+                            plane = shared_planes[4 * k : P, j * P - k * QUARTER : (j + 1) * P - k * QUARTER]
+                        else:
+                            plane = task_planes[4 * s : P, cols]
+                        nc.tensor.matmul_mx(
+                            out=z[:, i, :],
+                            lhsT=words[:, s, cols].bitcast(FP8X4),
+                            lhsT_scale=plane,
+                            rhs=x_codes[:, s, :].bitcast(FP8X4),
+                            rhs_scale=x_planes[:, s, :],
+                            start=True,
+                            stop=True,
+                        )
+                    for i in range(2):
+                        j = c * CHUNK_TILES + first + i
+                        bias = bias_cols[:, 1, j : j + 1] if s == SHARED else bias_cols[:, 0, 32 * s + j : 32 * s + j + 1]
+                        if vector_helps and first > 0:
+                            nc.vector.tensor_scalar(
+                                out=y[:, s, first + i, :], in0=z[:, i, :], scalar1=bias, scalar2=0.0, op0=ALU.add, op1=ALU.max
+                            )
+                        else:
+                            nc.scalar.activation(out=y[:, s, first + i, :], in_=z[:, i, :], func=ACT.Relu, bias=bias)
+
+        def transposed(y, h, s):
+            y_t = yt_pool.tile([P, CHUNK_TILES, P], F32, tag="yt")
+            for i in range(CHUNK_TILES):
+                nc.tensor.transpose(out=y_t[:, i, :], in_=y[:, s, i, h * P : (h + 1) * P], identity=identity[:])
+            return y_t[:].rearrange("p i (v e) -> p (i v) e", e=EXPERTS)
+
+        def weighted_sums(c, h, by_stream):
+            acc = acc_pool.tile([P, TASKS, CHUNK_UNITS], F32)
+            for g in range(GATES):
+                for t in range(TASKS):
+                    term = by_stream[t][:, :, g] if g < EXPERTS else by_stream[SHARED][:, :, g - EXPERTS]
+                    weight = gate[:, t * ROW_TILES + h, g : g + 1]
+                    if g == 0:
+                        nc.vector.tensor_scalar_mul(out=acc[:, t, :], in0=term, scalar1=weight)
+                    else:
+                        nc.vector.scalar_tensor_tensor(
+                            out=acc[:, t, :], in0=term, scalar=weight, in1=acc[:, t, :], op0=ALU.mult, op1=ALU.add
+                        )
+            nc.sync.dma_start(
+                out=out[:, h * P : (h + 1) * P, c * CHUNK_UNITS : (c + 1) * CHUNK_UNITS].rearrange("t p v -> p t v"),
+                in_=acc[:],
+            )
+
+        halves = [range(0, 2), range(2, STREAMS)]
+        y_of_chunk = [y_pool.tile([P, STREAMS, CHUNK_TILES, ROWS], F32, tag="y", name="y_first")]
+        experts(0, range(STREAMS), y_of_chunk[0], True)
+        by_stream = [transposed(y_of_chunk[0], 0, s) for s in range(STREAMS)]
+        for group in range(GROUPS):
+            c, h = divmod(group, ROW_TILES)
+            weighted_sums(c, h, by_stream)
+            if group + 1 == GROUPS:
+                break
+            if h == 0 and c + 1 < CHUNKS:
+                y_of_chunk.append(y_pool.tile([P, STREAMS, CHUNK_TILES, ROWS], F32, tag="y", name="y_next"))
+            next_c, next_h = divmod(group + 1, ROW_TILES)
+            by_stream = [transposed(y_of_chunk[next_c], next_h, 0)]
+            if c + 1 < CHUNKS:
+                experts(c + 1, halves[h], y_of_chunk[c + 1], False)
+            by_stream.extend(transposed(y_of_chunk[next_c], next_h, s) for s in range(1, STREAMS))

@@ -17,6 +17,7 @@ P = 128
 TASKS = 4
 STREAMS = TASKS + 1
 SHARED = TASKS
+NEED_ORDER = [0, 1, SHARED, 2, 3]
 ROWS = 256
 ROW_TILES = ROWS // P
 FEATURES = 512
@@ -66,9 +67,9 @@ def tile_plelayer_pb_e_kernel(
         )
 
         x_rows = keep.tile([P, STREAMS, ROW_TILES, FEATURES], BF16)
-        for t in range(TASKS):
-            nc.sync.dma_start(out=x_rows[:, t, :, :], in_=task_h[t].rearrange("(h p) u -> p h u", p=P))
-        nc.sync.dma_start(out=x_rows[:, SHARED, :, :], in_=share_h.rearrange("(h p) u -> p h u", p=P))
+        for s in NEED_ORDER:
+            rows = share_h if s == SHARED else task_h[s]
+            nc.sync.dma_start(out=x_rows[:, s, :, :], in_=rows.rearrange("(h p) u -> p h u", p=P))
 
         task_planes = keep.tile([P, COLS], U8, align_bytes=64)
         shared_planes = keep.tile([P, QUARTER], U8, align_bytes=64)
@@ -90,10 +91,9 @@ def tile_plelayer_pb_e_kernel(
         shared_words = ews1_words.rearrange("g p n k -> g p (n k)").bitcast(I32)
         for c in range(CHUNKS):
             cols = slice(c * CHUNK_COLS, (c + 1) * CHUNK_COLS)
-            nc.sync.dma_start(
-                out=words[:, 0:TASKS, cols].bitcast(I32), in_=task_words[:, :, cols].rearrange("t p n -> p t n")
-            )
-            nc.sync.dma_start(out=words[:, SHARED, cols].bitcast(I32), in_=shared_words[0, :, cols])
+            for s in NEED_ORDER:
+                packed = shared_words[0] if s == SHARED else task_words[s]
+                nc.sync.dma_start(out=words[:, s, cols].bitcast(I32), in_=packed[:, cols])
 
         bias_rows_f = keep.tile([P, 2, P], F32)
         nc.vector.tensor_copy(out=bias_rows_f[:], in_=bias_rows[:])
@@ -123,7 +123,7 @@ def tile_plelayer_pb_e_kernel(
         grouped = keep.tile([P, STREAMS, ROWS * 4], BF16, align_bytes=64)
         x_codes = keep.tile([P, STREAMS, ROWS], U32, align_bytes=64)
         x_planes = keep.tile([P, STREAMS, ROWS], U8, align_bytes=64)
-        for s in range(STREAMS):
+        for turn, s in enumerate(NEED_ORDER):
             x_t = z_pool.tile([P, 2, ROWS], F32, tag="z")
             for h in range(ROW_TILES):
                 x_words = x_rows[:, s, h, :].bitcast(F32)
@@ -134,16 +134,16 @@ def tile_plelayer_pb_e_kernel(
                         identity=identity[:],
                     )
             side_by_side = grouped[:, s, :].bitcast(F32).rearrange("p (b half) -> p b half", half=2)
-            if s % 2 == 0:
+            if turn % 2 == 0:
                 nc.vector.tensor_copy(out=side_by_side, in_=x_t[:].rearrange("p half b -> p b half"))
             else:
                 nc.scalar.copy(out=side_by_side, in_=x_t[:].rearrange("p half b -> p b half"))
-            for ready in [s - 2] if s < STREAMS - 1 else [s - 2, s - 1, s]:
+            for ready in [turn - 2] if turn < STREAMS - 1 else [turn - 2, turn - 1, turn]:
                 if ready >= 0:
                     nc.vector.quantize_mx(
-                        out=x_codes[:, ready, :].bitcast(FP8X4),
-                        scales=x_planes[:, ready, :],
-                        in_=grouped[:, ready, :],
+                        out=x_codes[:, NEED_ORDER[ready], :].bitcast(FP8X4),
+                        scales=x_planes[:, NEED_ORDER[ready], :],
+                        in_=grouped[:, NEED_ORDER[ready], :],
                     )
 
         total = keep.tile([P, pairs], F32)
@@ -155,36 +155,37 @@ def tile_plelayer_pb_e_kernel(
             out=gate[:], in0=powers[:], in1=inverse[:].unsqueeze(2).to_broadcast([P, pairs, GATES]), op=ALU.mult
         )
 
-        def experts(c, streams, y, vector_helps):
-            for s in streams:
-                for first in range(0, CHUNK_TILES, 2):
-                    z = z_pool.tile([P, 2, ROWS], F32, tag="z")
-                    for i in range(2):
-                        j = c * CHUNK_TILES + first + i
-                        cols = slice(j * P, (j + 1) * P)
-                        if s == SHARED:
-                            k = j * P // QUARTER
-                            plane = shared_planes[4 * k : P, j * P - k * QUARTER : (j + 1) * P - k * QUARTER]
-                        else:
-                            plane = task_planes[4 * s : P, cols]
-                        nc.tensor.matmul_mx(
-                            out=z[:, i, :],
-                            lhsT=words[:, s, cols].bitcast(FP8X4),
-                            lhsT_scale=plane,
-                            rhs=x_codes[:, s, :].bitcast(FP8X4),
-                            rhs_scale=x_planes[:, s, :],
-                            start=True,
-                            stop=True,
+        def experts(run, y, vector_helps):
+            c, place = divmod(run, STREAMS)
+            s = NEED_ORDER[place]
+            for first in range(0, CHUNK_TILES, 2):
+                z = z_pool.tile([P, 2, ROWS], F32, tag="z")
+                for i in range(2):
+                    j = c * CHUNK_TILES + first + i
+                    cols = slice(j * P, (j + 1) * P)
+                    if s == SHARED:
+                        k = j * P // QUARTER
+                        plane = shared_planes[4 * k : P, j * P - k * QUARTER : (j + 1) * P - k * QUARTER]
+                    else:
+                        plane = task_planes[4 * s : P, cols]
+                    nc.tensor.matmul_mx(
+                        out=z[:, i, :],
+                        lhsT=words[:, s, cols].bitcast(FP8X4),
+                        lhsT_scale=plane,
+                        rhs=x_codes[:, s, :].bitcast(FP8X4),
+                        rhs_scale=x_planes[:, s, :],
+                        start=True,
+                        stop=True,
+                    )
+                for i in range(2):
+                    j = c * CHUNK_TILES + first + i
+                    bias = bias_cols[:, 1, j : j + 1] if s == SHARED else bias_cols[:, 0, 32 * s + j : 32 * s + j + 1]
+                    if vector_helps and first > 0:
+                        nc.vector.tensor_scalar(
+                            out=y[:, s, first + i, :], in0=z[:, i, :], scalar1=bias, scalar2=0.0, op0=ALU.add, op1=ALU.max
                         )
-                    for i in range(2):
-                        j = c * CHUNK_TILES + first + i
-                        bias = bias_cols[:, 1, j : j + 1] if s == SHARED else bias_cols[:, 0, 32 * s + j : 32 * s + j + 1]
-                        if vector_helps and first > 0:
-                            nc.vector.tensor_scalar(
-                                out=y[:, s, first + i, :], in0=z[:, i, :], scalar1=bias, scalar2=0.0, op0=ALU.add, op1=ALU.max
-                            )
-                        else:
-                            nc.scalar.activation(out=y[:, s, first + i, :], in_=z[:, i, :], func=ACT.Relu, bias=bias)
+                    else:
+                        nc.scalar.activation(out=y[:, s, first + i, :], in_=z[:, i, :], func=ACT.Relu, bias=bias)
 
         def transposed(y, h, s):
             y_t = yt_pool.tile([P, CHUNK_TILES, P], F32, tag="yt")
@@ -192,36 +193,42 @@ def tile_plelayer_pb_e_kernel(
                 nc.tensor.transpose(out=y_t[:, i, :], in_=y[:, s, i, h * P : (h + 1) * P], identity=identity[:])
             return y_t[:].rearrange("p i (v e) -> p (i v) e", e=EXPERTS)
 
-        def weighted_sums(c, h, by_stream):
-            acc = acc_pool.tile([P, TASKS, CHUNK_UNITS], F32)
-            for g in range(GATES):
+        def weighted_sums(h, late, by_stream, acc):
+            for e in range(EXPERTS):
                 for t in range(TASKS):
-                    term = by_stream[t][:, :, g] if g < EXPERTS else by_stream[SHARED][:, :, g - EXPERTS]
+                    own = (t < TASKS // 2) != late
+                    term = by_stream[t][:, :, e] if own else by_stream[SHARED][:, :, e]
+                    g = e if own else EXPERTS + e
                     weight = gate[:, t * ROW_TILES + h, g : g + 1]
-                    if g == 0:
-                        nc.vector.tensor_scalar_mul(out=acc[:, t, :], in0=term, scalar1=weight)
+                    part = acc[:, e % 2, t, :]
+                    if e < 2 and not late:
+                        nc.scalar.activation(out=part, in_=term, func=ACT.Copy, scale=weight)
                     else:
                         nc.vector.scalar_tensor_tensor(
-                            out=acc[:, t, :], in0=term, scalar=weight, in1=acc[:, t, :], op0=ALU.mult, op1=ALU.add
+                            out=part, in0=term, scalar=weight, in1=part, op0=ALU.mult, op1=ALU.add
                         )
-            nc.sync.dma_start(
-                out=out[:, h * P : (h + 1) * P, c * CHUNK_UNITS : (c + 1) * CHUNK_UNITS].rearrange("t p v -> p t v"),
-                in_=acc[:],
-            )
 
-        halves = [range(0, 2), range(2, STREAMS)]
         y_of_chunk = [y_pool.tile([P, STREAMS, CHUNK_TILES, ROWS], F32, tag="y", name="y_first")]
-        experts(0, range(STREAMS), y_of_chunk[0], True)
-        by_stream = [transposed(y_of_chunk[0], 0, s) for s in range(STREAMS)]
-        for group in range(GROUPS):
-            c, h = divmod(group, ROW_TILES)
-            weighted_sums(c, h, by_stream)
-            if group + 1 == GROUPS:
-                break
-            if h == 0 and c + 1 < CHUNKS:
-                y_of_chunk.append(y_pool.tile([P, STREAMS, CHUNK_TILES, ROWS], F32, tag="y", name="y_next"))
-            next_c, next_h = divmod(group + 1, ROW_TILES)
-            by_stream = [transposed(y_of_chunk[next_c], next_h, 0)]
+        for run in range(STREAMS):
+            experts(run, y_of_chunk[0], True)
+        by_stream = {}
+        for c in range(CHUNKS):
             if c + 1 < CHUNKS:
-                experts(c + 1, halves[h], y_of_chunk[c + 1], False)
-            by_stream.extend(transposed(y_of_chunk[next_c], next_h, s) for s in range(1, STREAMS))
+                y_of_chunk.append(y_pool.tile([P, STREAMS, CHUNK_TILES, ROWS], F32, tag="y", name="y_next"))
+            for step in range(STREAMS):
+                for bank in (2 * step, 2 * step + 1):
+                    h, place = divmod(bank, STREAMS)
+                    by_stream[NEED_ORDER[place]] = transposed(y_of_chunk[c], h, NEED_ORDER[place])
+                    if place == 2:
+                        acc = acc_pool.tile([P, 2, TASKS, CHUNK_UNITS], F32)
+                        weighted_sums(h, False, by_stream, acc)
+                    if place == 4:
+                        weighted_sums(h, True, by_stream, acc)
+                        result = acc_pool.tile([P, TASKS, CHUNK_UNITS], F32)
+                        nc.gpsimd.tensor_tensor(out=result[:], in0=acc[:, 0, :, :], in1=acc[:, 1, :, :], op=ALU.add)
+                        units = slice(c * CHUNK_UNITS, (c + 1) * CHUNK_UNITS)
+                        nc.sync.dma_start(
+                            out=out[:, h * P : (h + 1) * P, units].rearrange("t p v -> p t v"), in_=result[:]
+                        )
+                if c + 1 < CHUNKS:
+                    experts((c + 1) * STREAMS + step, y_of_chunk[c + 1], False)

@@ -160,6 +160,16 @@ def tile_plelayer_pb_e_kernel(
             s = NEED_ORDER[place]
             for first in range(0, CHUNK_TILES, 2):
                 z = z_pool.tile([P, 2, ROWS], F32, tag="z")
+                if first == 0:
+                    nc.tensor.matmul_mx(
+                        out=z[:].rearrange("p i b -> p (i b)"),
+                        lhsT=words[:, s, 0:P].bitcast(FP8X4),
+                        lhsT_scale=shared_planes[:, 0:P],
+                        rhs=x_codes[:, 0:2, :].rearrange("p s b -> p (s b)").bitcast(FP8X4),
+                        rhs_scale=x_planes[:, 0:2, :].rearrange("p s b -> p (s b)"),
+                        start=True,
+                        stop=True,
+                    )
                 for i in range(2):
                     j = c * CHUNK_TILES + first + i
                     cols = slice(j * P, (j + 1) * P)

@@ -31,6 +31,11 @@ CHUNK_COLS = CHUNK_TILES * P
 CHUNK_UNITS = CHUNK_COLS // EXPERTS
 CHUNKS = COLS // CHUNK_COLS
 GROUPS = CHUNKS * ROW_TILES
+RUNS = CHUNKS * STREAMS
+JOBS = GROUPS * TASKS
+JOB_ROUNDS = GATES // 2
+STAGGER = 2
+OWN_BANKS = 4
 QUARTER = COLS // 4
 
 FLOPS = 2 * STREAMS * ROWS * FEATURES * COLS
@@ -44,9 +49,11 @@ def tile_plelayer_pb_e_kernel(
         stack.enter_context(tc.manual_schedule())
         keep = stack.enter_context(tc.tile_pool(name="keep", bufs=1))
         y_pool = stack.enter_context(tc.tile_pool(name="y", bufs=2))
-        acc_pool = stack.enter_context(tc.tile_pool(name="acc", bufs=4))
+        acc_pool = stack.enter_context(tc.tile_pool(name="acc", bufs=12))
+        result_pool = stack.enter_context(tc.tile_pool(name="result", bufs=3))
         z_pool = stack.enter_context(tc.psum_pool(name="z", bufs=2))
-        yt_pool = stack.enter_context(tc.psum_pool(name="yt", bufs=6))
+        own_pool = stack.enter_context(tc.psum_pool(name="own", bufs=OWN_BANKS))
+        shared_pool = stack.enter_context(tc.psum_pool(name="shared", bufs=2))
 
         identity = keep.tile([P, P], F32)
         make_identity(nc, identity[:])
@@ -155,21 +162,16 @@ def tile_plelayer_pb_e_kernel(
             out=gate[:], in0=powers[:], in1=inverse[:].unsqueeze(2).to_broadcast([P, pairs, GATES]), op=ALU.mult
         )
 
-        def experts(run, y, vector_helps):
+        y_of_chunk = []
+
+        def experts(run, vector_helps):
             c, place = divmod(run, STREAMS)
             s = NEED_ORDER[place]
+            if place == 0:
+                y_of_chunk.append(y_pool.tile([P, STREAMS, CHUNK_TILES, ROWS], F32, tag="y", name="y"))
+            y = y_of_chunk[c]
             for first in range(0, CHUNK_TILES, 2):
                 z = z_pool.tile([P, 2, ROWS], F32, tag="z")
-                if first == 0:
-                    nc.tensor.matmul_mx(
-                        out=z[:].rearrange("p i b -> p (i b)"),
-                        lhsT=words[:, s, 0:P].bitcast(FP8X4),
-                        lhsT_scale=shared_planes[:, 0:P],
-                        rhs=x_codes[:, 0:2, :].rearrange("p s b -> p (s b)").bitcast(FP8X4),
-                        rhs_scale=x_planes[:, 0:2, :].rearrange("p s b -> p (s b)"),
-                        start=True,
-                        stop=True,
-                    )
                 for i in range(2):
                     j = c * CHUNK_TILES + first + i
                     cols = slice(j * P, (j + 1) * P)
@@ -197,48 +199,78 @@ def tile_plelayer_pb_e_kernel(
                     else:
                         nc.scalar.activation(out=y[:, s, first + i, :], in_=z[:, i, :], func=ACT.Relu, bias=bias)
 
-        def transposed(y, h, s):
-            y_t = yt_pool.tile([P, CHUNK_TILES, P], F32, tag="yt")
+        own_terms = {}
+        shared_terms = {}
+        sums = {}
+        results = {}
+
+        def bank(group, s):
+            c, h = divmod(group, ROW_TILES)
+            if s == SHARED:
+                y_t = shared_pool.tile([P, CHUNK_TILES, P], F32, tag="shared")
+            else:
+                y_t = own_pool.tile([P, CHUNK_TILES, P], F32, tag="own")
             for i in range(CHUNK_TILES):
-                nc.tensor.transpose(out=y_t[:, i, :], in_=y[:, s, i, h * P : (h + 1) * P], identity=identity[:])
-            return y_t[:].rearrange("p i (v e) -> p (i v) e", e=EXPERTS)
+                nc.tensor.transpose(
+                    out=y_t[:, i, :], in_=y_of_chunk[c][:, s, i, h * P : (h + 1) * P], identity=identity[:]
+                )
+            terms = y_t[:].rearrange("p i (v e) -> p (i v) e", e=EXPERTS)
+            if s == SHARED:
+                shared_terms[group] = terms
+            else:
+                job = group * TASKS + s
+                own_terms[job] = terms
+                sums[job] = acc_pool.tile([P, 2, CHUNK_UNITS], F32, tag="acc", name="acc")
+                for parity in range(2):
+                    nc.scalar.activation(
+                        out=sums[job][:, parity, :],
+                        in_=terms[:, :, parity],
+                        func=ACT.Copy,
+                        scale=gate[:, s * ROW_TILES + h, parity : parity + 1],
+                    )
+            number = group * STREAMS + NEED_ORDER.index(s)
+            if number % 2 == 1 and STREAMS + number // 2 < RUNS:
+                experts(STREAMS + number // 2, False)
 
-        def weighted_sums(h, late, by_stream, acc):
-            for e in range(EXPERTS):
-                for t in range(TASKS):
-                    own = (t < TASKS // 2) != late
-                    term = by_stream[t][:, :, e] if own else by_stream[SHARED][:, :, e]
-                    g = e if own else EXPERTS + e
-                    weight = gate[:, t * ROW_TILES + h, g : g + 1]
-                    part = acc[:, e % 2, t, :]
-                    if e < 2 and not late:
-                        nc.scalar.activation(out=part, in_=term, func=ACT.Copy, scale=weight)
-                    else:
-                        nc.vector.scalar_tensor_tensor(
-                            out=part, in0=term, scalar=weight, in1=part, op0=ALU.mult, op1=ALU.add
-                        )
-
-        y_of_chunk = [y_pool.tile([P, STREAMS, CHUNK_TILES, ROWS], F32, tag="y", name="y_first")]
         for run in range(STREAMS):
-            experts(run, y_of_chunk[0], True)
-        by_stream = {}
-        for c in range(CHUNKS):
-            if c + 1 < CHUNKS:
-                y_of_chunk.append(y_pool.tile([P, STREAMS, CHUNK_TILES, ROWS], F32, tag="y", name="y_next"))
-            for step in range(STREAMS):
-                for bank in (2 * step, 2 * step + 1):
-                    h, place = divmod(bank, STREAMS)
-                    by_stream[NEED_ORDER[place]] = transposed(y_of_chunk[c], h, NEED_ORDER[place])
-                    if place == 2:
-                        acc = acc_pool.tile([P, 2, TASKS, CHUNK_UNITS], F32)
-                        weighted_sums(h, False, by_stream, acc)
-                    if place == 4:
-                        weighted_sums(h, True, by_stream, acc)
-                        result = acc_pool.tile([P, TASKS, CHUNK_UNITS], F32)
-                        nc.gpsimd.tensor_tensor(out=result[:], in0=acc[:, 0, :, :], in1=acc[:, 1, :, :], op=ALU.add)
+            experts(run, True)
+        for s in NEED_ORDER:
+            bank(0, s)
+
+        for r in range(STAGGER * (JOBS - 1) + JOB_ROUNDS):
+            for job in range(JOBS):
+                step = r - STAGGER * job
+                if step < 1 or step >= JOB_ROUNDS:
+                    continue
+                group, t = divmod(job, TASKS)
+                c, h = divmod(group, ROW_TILES)
+                for parity in range(2):
+                    e = (2 * step + parity) % EXPERTS
+                    own = step < JOB_ROUNDS // 2
+                    g = e if own else EXPERTS + e
+                    nc.vector.scalar_tensor_tensor(
+                        out=sums[job][:, parity, :],
+                        in0=own_terms[job][:, :, e] if own else shared_terms[group][:, :, e],
+                        scalar=gate[:, t * ROW_TILES + h, g : g + 1],
+                        in1=sums[job][:, parity, :],
+                        op0=ALU.mult,
+                        op1=ALU.add,
+                    )
+                if step == JOB_ROUNDS - 1:
+                    if t == 0:
+                        results[group] = result_pool.tile([P, TASKS, CHUNK_UNITS], F32, tag="result", name="result")
+                    nc.gpsimd.tensor_tensor(
+                        out=results[group][:, t, :], in0=sums[job][:, 0, :], in1=sums[job][:, 1, :], op=ALU.add
+                    )
+                    if t == TASKS - 1:
                         units = slice(c * CHUNK_UNITS, (c + 1) * CHUNK_UNITS)
                         nc.sync.dma_start(
-                            out=out[:, h * P : (h + 1) * P, units].rearrange("t p v -> p t v"), in_=result[:]
+                            out=out[:, h * P : (h + 1) * P, units].rearrange("t p v -> p t v"), in_=results[group][:]
                         )
-                if c + 1 < CHUNKS:
-                    experts((c + 1) * STREAMS + step, y_of_chunk[c + 1], False)
+            done_with_own_bank, odd = divmod(r - (JOB_ROUNDS // 2 - 1), STAGGER)
+            job = done_with_own_bank + OWN_BANKS
+            if odd == 0 and done_with_own_bank >= 0 and job < JOBS:
+                group, t = divmod(job, TASKS)
+                if NEED_ORDER[NEED_ORDER.index(t) - 1] == SHARED:
+                    bank(group, SHARED)
+                bank(group, t)

@@ -102,6 +102,12 @@ def tile_plelayer_pb_e_kernel(
                 packed = shared_words[0] if s == SHARED else task_words[s]
                 nc.sync.dma_start(out=words[:, s, cols].bitcast(I32), in_=packed[:, cols])
 
+        by_expert = keep.tile([P, P], F32)
+        nc.vector.tensor_copy(
+            out=by_expert[:].rearrange("p (e v) -> p e v", e=EXPERTS),
+            in_=identity[:].rearrange("p (v e) -> p e v", e=EXPERTS),
+        )
+
         bias_rows_f = keep.tile([P, 2, P], F32)
         nc.vector.tensor_copy(out=bias_rows_f[:], in_=bias_rows[:])
         bias_t = z_pool.tile([P, 2, P], F32, tag="z")
@@ -212,19 +218,19 @@ def tile_plelayer_pb_e_kernel(
                 y_t = own_pool.tile([P, CHUNK_TILES, P], F32, tag="own")
             for i in range(CHUNK_TILES):
                 nc.tensor.transpose(
-                    out=y_t[:, i, :], in_=y_of_chunk[c][:, s, i, h * P : (h + 1) * P], identity=identity[:]
+                    out=y_t[:, i, :], in_=y_of_chunk[c][:, s, i, h * P : (h + 1) * P], identity=by_expert[:]
                 )
-            terms = y_t[:].rearrange("p i (v e) -> p (i v) e", e=EXPERTS)
+            terms = y_t[:].rearrange("p i (e v) -> p e i v", e=EXPERTS)
             if s == SHARED:
                 shared_terms[group] = terms
             else:
                 job = group * TASKS + s
                 own_terms[job] = terms
-                sums[job] = acc_pool.tile([P, 2, CHUNK_UNITS], F32, tag="acc", name="acc")
+                sums[job] = acc_pool.tile([P, 2, CHUNK_TILES, CHUNK_UNITS // CHUNK_TILES], F32, tag="acc", name="acc")
                 for parity in range(2):
                     nc.scalar.activation(
-                        out=sums[job][:, parity, :],
-                        in_=terms[:, :, parity],
+                        out=sums[job][:, parity, :, :],
+                        in_=terms[:, parity, :, :],
                         func=ACT.Copy,
                         scale=gate[:, s * ROW_TILES + h, parity : parity + 1],
                     )
@@ -249,10 +255,10 @@ def tile_plelayer_pb_e_kernel(
                     own = step < JOB_ROUNDS // 2
                     g = e if own else EXPERTS + e
                     nc.vector.scalar_tensor_tensor(
-                        out=sums[job][:, parity, :],
-                        in0=own_terms[job][:, :, e] if own else shared_terms[group][:, :, e],
+                        out=sums[job][:, parity, :, :],
+                        in0=own_terms[job][:, e, :, :] if own else shared_terms[group][:, e, :, :],
                         scalar=gate[:, t * ROW_TILES + h, g : g + 1],
-                        in1=sums[job][:, parity, :],
+                        in1=sums[job][:, parity, :, :],
                         op0=ALU.mult,
                         op1=ALU.add,
                     )
@@ -260,7 +266,10 @@ def tile_plelayer_pb_e_kernel(
                     if t == 0:
                         results[group] = result_pool.tile([P, TASKS, CHUNK_UNITS], F32, tag="result", name="result")
                     nc.gpsimd.tensor_tensor(
-                        out=results[group][:, t, :], in0=sums[job][:, 0, :], in1=sums[job][:, 1, :], op=ALU.add
+                        out=results[group][:, t, :],
+                        in0=sums[job][:, 0, :, :].rearrange("p i v -> p (i v)"),
+                        in1=sums[job][:, 1, :, :].rearrange("p i v -> p (i v)"),
+                        op=ALU.add,
                     )
                     if t == TASKS - 1:
                         units = slice(c * CHUNK_UNITS, (c + 1) * CHUNK_UNITS)

@@ -33,8 +33,9 @@ CHUNKS = COLS // CHUNK_COLS
 GROUPS = CHUNKS * ROW_TILES
 RUNS = CHUNKS * STREAMS
 JOBS = GROUPS * TASKS
-JOB_ROUNDS = GATES // 2
-STAGGER = 2
+PARTS = 4
+JOB_ROUNDS = GATES // PARTS
+STAGGER = 1
 OWN_BANKS = 4
 QUARTER = COLS // 4
 
@@ -226,13 +227,13 @@ def tile_plelayer_pb_e_kernel(
             else:
                 job = group * TASKS + s
                 own_terms[job] = terms
-                sums[job] = acc_pool.tile([P, 2, CHUNK_TILES, CHUNK_UNITS // CHUNK_TILES], F32, tag="acc", name="acc")
-                for parity in range(2):
+                sums[job] = acc_pool.tile([P, PARTS, CHUNK_TILES, CHUNK_UNITS // CHUNK_TILES], F32, tag="acc", name="acc")
+                for part in range(PARTS):
                     nc.scalar.activation(
-                        out=sums[job][:, parity, :, :],
-                        in_=terms[:, parity, :, :],
+                        out=sums[job][:, part, :, :],
+                        in_=terms[:, part, :, :],
                         func=ACT.Copy,
-                        scale=gate[:, s * ROW_TILES + h, parity : parity + 1],
+                        scale=gate[:, s * ROW_TILES + h, part : part + 1],
                     )
             number = group * STREAMS + NEED_ORDER.index(s)
             if number % 2 == 1 and STREAMS + number // 2 < RUNS:
@@ -250,21 +251,24 @@ def tile_plelayer_pb_e_kernel(
                     continue
                 group, t = divmod(job, TASKS)
                 c, h = divmod(group, ROW_TILES)
-                for parity in range(2):
-                    e = (2 * step + parity) % EXPERTS
+                for part in range(PARTS):
+                    e = (PARTS * step + part) % EXPERTS
                     own = step < JOB_ROUNDS // 2
                     g = e if own else EXPERTS + e
                     nc.vector.scalar_tensor_tensor(
-                        out=sums[job][:, parity, :, :],
+                        out=sums[job][:, part, :, :],
                         in0=own_terms[job][:, e, :, :] if own else shared_terms[group][:, e, :, :],
                         scalar=gate[:, t * ROW_TILES + h, g : g + 1],
-                        in1=sums[job][:, parity, :, :],
+                        in1=sums[job][:, part, :, :],
                         op0=ALU.mult,
                         op1=ALU.add,
                     )
                 if step == JOB_ROUNDS - 1:
                     if t == 0:
                         results[group] = result_pool.tile([P, TASKS, CHUNK_UNITS], F32, tag="result", name="result")
+                    nc.gpsimd.tensor_tensor(
+                        out=sums[job][:, 0:2, :, :], in0=sums[job][:, 0:2, :, :], in1=sums[job][:, 2:4, :, :], op=ALU.add
+                    )
                     nc.gpsimd.tensor_tensor(
                         out=results[group][:, t, :],
                         in0=sums[job][:, 0, :, :].rearrange("p i v -> p (i v)"),

@@ -36,6 +36,7 @@ JOBS = GROUPS * TASKS
 PARTS = 4
 JOB_ROUNDS = GATES // PARTS
 STAGGER = 1
+VECTOR_STARTS = 8
 OWN_BANKS = 4
 QUARTER = COLS // 4
 
@@ -228,13 +229,14 @@ def tile_plelayer_pb_e_kernel(
                 job = group * TASKS + s
                 own_terms[job] = terms
                 sums[job] = acc_pool.tile([P, PARTS, CHUNK_TILES, CHUNK_UNITS // CHUNK_TILES], F32, tag="acc", name="acc")
-                for part in range(PARTS):
-                    nc.scalar.activation(
-                        out=sums[job][:, part, :, :],
-                        in_=terms[:, part, :, :],
-                        func=ACT.Copy,
-                        scale=gate[:, s * ROW_TILES + h, part : part + 1],
-                    )
+                if job % VECTOR_STARTS > 0:
+                    for part in range(PARTS):
+                        nc.scalar.activation(
+                            out=sums[job][:, part, :, :],
+                            in_=terms[:, part, :, :],
+                            func=ACT.Copy,
+                            scale=gate[:, s * ROW_TILES + h, part : part + 1],
+                        )
             number = group * STREAMS + NEED_ORDER.index(s)
             if number % 2 == 1 and STREAMS + number // 2 < RUNS:
                 experts(STREAMS + number // 2, False)
@@ -247,10 +249,22 @@ def tile_plelayer_pb_e_kernel(
         for r in range(STAGGER * (JOBS - 1) + JOB_ROUNDS):
             for job in range(JOBS):
                 step = r - STAGGER * job
-                if step < 1 or step >= JOB_ROUNDS:
+                if step < 0 or step >= JOB_ROUNDS:
                     continue
                 group, t = divmod(job, TASKS)
                 c, h = divmod(group, ROW_TILES)
+                if step == 0:
+                    if job % VECTOR_STARTS == 0:
+                        nc.vector.tensor_tensor(
+                            out=sums[job][:],
+                            in0=own_terms[job][:, 0:PARTS, :, :],
+                            in1=gate[:, t * ROW_TILES + h, 0:PARTS]
+                            .unsqueeze(2)
+                            .unsqueeze(3)
+                            .to_broadcast([P, PARTS, CHUNK_TILES, CHUNK_UNITS // CHUNK_TILES]),
+                            op=ALU.mult,
+                        )
+                    continue
                 for part in range(PARTS):
                     e = (PARTS * step + part) % EXPERTS
                     own = step < JOB_ROUNDS // 2

@@ -37,7 +37,7 @@ PARTS = 4
 JOB_ROUNDS = GATES // PARTS
 STAGGER = 1
 VECTOR_STARTS = 8
-OWN_BANKS = 4
+OWN_BANKS = 3
 QUARTER = COLS // 4
 
 FLOPS = 2 * STREAMS * ROWS * FEATURES * COLS
@@ -53,7 +53,7 @@ def tile_plelayer_pb_e_kernel(
         y_pool = stack.enter_context(tc.tile_pool(name="y", bufs=2))
         acc_pool = stack.enter_context(tc.tile_pool(name="acc", bufs=12))
         result_pool = stack.enter_context(tc.tile_pool(name="result", bufs=3))
-        z_pool = stack.enter_context(tc.psum_pool(name="z", bufs=2))
+        z_pool = stack.enter_context(tc.psum_pool(name="z", bufs=3))
         own_pool = stack.enter_context(tc.psum_pool(name="own", bufs=OWN_BANKS))
         shared_pool = stack.enter_context(tc.psum_pool(name="shared", bufs=2))
 
@@ -243,7 +243,7 @@ def tile_plelayer_pb_e_kernel(
 
         for run in range(STREAMS):
             experts(run, True)
-        for s in NEED_ORDER:
+        for s in NEED_ORDER[: OWN_BANKS + 1]:
             bank(0, s)
 
         for r in range(STAGGER * (JOBS - 1) + JOB_ROUNDS):

@@ -28,6 +28,7 @@ COL_TILES = COLS // P
 GATES = 2 * EXPERTS
 CHUNK_TILES = 4
 CHUNK_COLS = CHUNK_TILES * P
+UNITS_PER_TILE = P // EXPERTS
 CHUNK_UNITS = CHUNK_COLS // EXPERTS
 CHUNKS = COLS // CHUNK_COLS
 GROUPS = CHUNKS * ROW_TILES
@@ -215,25 +216,25 @@ def tile_plelayer_pb_e_kernel(
         def bank(group, s):
             c, h = divmod(group, ROW_TILES)
             if s == SHARED:
-                y_t = shared_pool.tile([P, CHUNK_TILES, P], F32, tag="shared")
+                y_t = shared_pool.tile([P, EXPERTS, CHUNK_TILES, UNITS_PER_TILE], F32, tag="shared")
             else:
-                y_t = own_pool.tile([P, CHUNK_TILES, P], F32, tag="own")
+                y_t = own_pool.tile([P, EXPERTS, CHUNK_TILES, UNITS_PER_TILE], F32, tag="own")
             for i in range(CHUNK_TILES):
                 nc.tensor.transpose(
-                    out=y_t[:, i, :], in_=y_of_chunk[c][:, s, i, h * P : (h + 1) * P], identity=by_expert[:]
+                    out=y_t[:, :, i, :], in_=y_of_chunk[c][:, s, i, h * P : (h + 1) * P], identity=by_expert[:]
                 )
-            terms = y_t[:].rearrange("p i (e v) -> p e i v", e=EXPERTS)
+            terms = y_t[:].rearrange("p e i v -> p e (i v)")
             if s == SHARED:
                 shared_terms[group] = terms
             else:
                 job = group * TASKS + s
                 own_terms[job] = terms
-                sums[job] = acc_pool.tile([P, PARTS, CHUNK_TILES, CHUNK_UNITS // CHUNK_TILES], F32, tag="acc", name="acc")
+                sums[job] = acc_pool.tile([P, PARTS, CHUNK_UNITS], F32, tag="acc", name="acc")
                 if job % VECTOR_STARTS > 0:
                     for part in range(PARTS):
                         nc.scalar.activation(
-                            out=sums[job][:, part, :, :],
-                            in_=terms[:, part, :, :],
+                            out=sums[job][:, part, :],
+                            in_=terms[:, part, :],
                             func=ACT.Copy,
                             scale=gate[:, s * ROW_TILES + h, part : part + 1],
                         )
@@ -257,11 +258,10 @@ def tile_plelayer_pb_e_kernel(
                     if job % VECTOR_STARTS == 0:
                         nc.vector.tensor_tensor(
                             out=sums[job][:],
-                            in0=own_terms[job][:, 0:PARTS, :, :],
+                            in0=own_terms[job][:, 0:PARTS, :],
                             in1=gate[:, t * ROW_TILES + h, 0:PARTS]
                             .unsqueeze(2)
-                            .unsqueeze(3)
-                            .to_broadcast([P, PARTS, CHUNK_TILES, CHUNK_UNITS // CHUNK_TILES]),
+                            .to_broadcast([P, PARTS, CHUNK_UNITS]),
                             op=ALU.mult,
                         )
                     continue
@@ -270,10 +270,10 @@ def tile_plelayer_pb_e_kernel(
                     own = step < JOB_ROUNDS // 2
                     g = e if own else EXPERTS + e
                     nc.vector.scalar_tensor_tensor(
-                        out=sums[job][:, part, :, :],
-                        in0=own_terms[job][:, e, :, :] if own else shared_terms[group][:, e, :, :],
+                        out=sums[job][:, part, :],
+                        in0=own_terms[job][:, e, :] if own else shared_terms[group][:, e, :],
                         scalar=gate[:, t * ROW_TILES + h, g : g + 1],
-                        in1=sums[job][:, part, :, :],
+                        in1=sums[job][:, part, :],
                         op0=ALU.mult,
                         op1=ALU.add,
                     )
@@ -281,12 +281,12 @@ def tile_plelayer_pb_e_kernel(
                     if t == 0:
                         results[group] = result_pool.tile([P, TASKS, CHUNK_UNITS], F32, tag="result", name="result")
                     nc.gpsimd.tensor_tensor(
-                        out=sums[job][:, 0:2, :, :], in0=sums[job][:, 0:2, :, :], in1=sums[job][:, 2:4, :, :], op=ALU.add
+                        out=sums[job][:, 0:2, :], in0=sums[job][:, 0:2, :], in1=sums[job][:, 2:4, :], op=ALU.add
                     )
                     nc.gpsimd.tensor_tensor(
                         out=results[group][:, t, :],
-                        in0=sums[job][:, 0, :, :].rearrange("p i v -> p (i v)"),
-                        in1=sums[job][:, 1, :, :].rearrange("p i v -> p (i v)"),
+                        in0=sums[job][:, 0, :],
+                        in1=sums[job][:, 1, :],
                         op=ALU.add,
                     )
                     if t == TASKS - 1:

@@ -239,10 +239,15 @@ def tile_plelayer_pb_e_kernel(
                             scale=gate[:, s * ROW_TILES + h, part : part + 1],
                         )
             number = group * STREAMS + NEED_ORDER.index(s)
-            if number % 2 == 1 and STREAMS + number // 2 < RUNS:
-                experts(STREAMS + number // 2, False)
+            for run in runs_behind.get(number, []):
+                experts(run, False)
 
-        for run in range(STREAMS):
+        runs_behind = {}
+        for run in range(4, RUNS):
+            place = run - 4 if run < STREAMS else 2 * (run - STREAMS) + 1 + 2
+            runs_behind.setdefault(place, []).append(run)
+
+        for run in range(4):
             experts(run, True)
         for s in NEED_ORDER[: OWN_BANKS + 1]:
             bank(0, s)
@@ -280,19 +285,22 @@ def tile_plelayer_pb_e_kernel(
                 if step == JOB_ROUNDS - 1:
                     if t == 0:
                         results[group] = result_pool.tile([P, TASKS, CHUNK_UNITS], F32, tag="result", name="result")
-                    nc.gpsimd.tensor_tensor(
+                    joiner = nc.vector if job >= JOBS - 1 else nc.gpsimd
+                    joiner.tensor_tensor(
                         out=sums[job][:, 0:2, :], in0=sums[job][:, 0:2, :], in1=sums[job][:, 2:4, :], op=ALU.add
                     )
-                    nc.gpsimd.tensor_tensor(
+                    joiner.tensor_tensor(
                         out=results[group][:, t, :],
                         in0=sums[job][:, 0, :],
                         in1=sums[job][:, 1, :],
                         op=ALU.add,
                     )
-                    if t == TASKS - 1:
+                    tasks = slice(t, t + 1) if group == GROUPS - 1 else slice(0, TASKS)
+                    if t == TASKS - 1 or group == GROUPS - 1:
                         units = slice(c * CHUNK_UNITS, (c + 1) * CHUNK_UNITS)
                         nc.sync.dma_start(
-                            out=out[:, h * P : (h + 1) * P, units].rearrange("t p v -> p t v"), in_=results[group][:]
+                            out=out[tasks, h * P : (h + 1) * P, units].rearrange("t p v -> p t v"),
+                            in_=results[group][:, tasks, :],
                         )
             done_with_own_bank, odd = divmod(r - (JOB_ROUNDS // 2 - 1), STAGGER)
             job = done_with_own_bank + OWN_BANKS

@@ -37,7 +37,7 @@ JOBS = GROUPS * TASKS
 PARTS = 4
 JOB_ROUNDS = GATES // PARTS
 STAGGER = 1
-VECTOR_STARTS = 8
+VECTOR_STARTS = 7
 OWN_BANKS = 3
 QUARTER = COLS // 4
 
@@ -208,6 +208,9 @@ def tile_plelayer_pb_e_kernel(
                     else:
                         nc.scalar.activation(out=y[:, s, first + i, :], in_=z[:, i, :], func=ACT.Relu, bias=bias)
 
+        def vector_starts(job):
+            return job % VECTOR_STARTS == 0 and job < (CHUNKS - 1) * ROW_TILES * TASKS
+
         own_terms = {}
         shared_terms = {}
         sums = {}
@@ -230,7 +233,7 @@ def tile_plelayer_pb_e_kernel(
                 job = group * TASKS + s
                 own_terms[job] = terms
                 sums[job] = acc_pool.tile([P, PARTS, CHUNK_UNITS], F32, tag="acc", name="acc")
-                if job % VECTOR_STARTS > 0:
+                if not vector_starts(job):
                     for part in range(PARTS):
                         nc.scalar.activation(
                             out=sums[job][:, part, :],
@@ -260,7 +263,7 @@ def tile_plelayer_pb_e_kernel(
                 group, t = divmod(job, TASKS)
                 c, h = divmod(group, ROW_TILES)
                 if step == 0:
-                    if job % VECTOR_STARTS == 0:
+                    if vector_starts(job):
                         nc.vector.tensor_tensor(
                             out=sums[job][:],
                             in0=own_terms[job][:, 0:PARTS, :],

from contextlib import ExitStack

import concourse.mybir as mybir
from concourse.masks import make_identity

F32 = mybir.dt.float32
BF16 = mybir.dt.bfloat16
I32 = mybir.dt.int32
U32 = mybir.dt.uint32
U8 = mybir.dt.uint8
FP8X4 = mybir.dt.float8_e4m3fn_x4
ALU = mybir.AluOpType
ACT = mybir.ActivationFunctionType
AX = mybir.AxisListType

P = 128
TASKS = 4
STREAMS = TASKS + 1
SHARED = TASKS
NEED_ORDER = [0, 1, SHARED, 2, 3]
ROWS = 256
ROW_TILES = ROWS // P
FEATURES = 512
UNITS = 512
EXPERTS = 8
COLS = UNITS * EXPERTS
COL_TILES = COLS // P
GATES = 2 * EXPERTS
CHUNK_TILES = 4
CHUNK_COLS = CHUNK_TILES * P
UNITS_PER_TILE = P // EXPERTS
CHUNK_UNITS = CHUNK_COLS // EXPERTS
CHUNKS = COLS // CHUNK_COLS
GROUPS = CHUNKS * ROW_TILES
RUNS = CHUNKS * STREAMS
JOBS = GROUPS * TASKS
PARTS = 4
JOB_ROUNDS = GATES // PARTS
STAGGER = 1
VECTOR_STARTS = 7
OWN_BANKS = 3
QUARTER = COLS // 4

FLOPS = 2 * STREAMS * ROWS * FEATURES * COLS


def tile_plelayer_pb_e_kernel(
    tc, task_h, share_h, ews1_words, ews1_scales, ebs1, ew1_words, ew1_scales, eb1, gate_pre1, gb1, out
):
    nc = tc.nc
    with ExitStack() as stack:
        stack.enter_context(tc.manual_schedule())
        keep = stack.enter_context(tc.tile_pool(name="keep", bufs=1))
        y_pool = stack.enter_context(tc.tile_pool(name="y", bufs=2))
        acc_pool = stack.enter_context(tc.tile_pool(name="acc", bufs=12))
        result_pool = stack.enter_context(tc.tile_pool(name="result", bufs=3))
        z_pool = stack.enter_context(tc.psum_pool(name="z", bufs=3))
        own_pool = stack.enter_context(tc.psum_pool(name="own", bufs=OWN_BANKS))
        shared_pool = stack.enter_context(tc.psum_pool(name="shared", bufs=2))

        identity = keep.tile([P, P], F32)
        make_identity(nc, identity[:])

        bias_rows = keep.tile([P, 2, P], BF16)
        nc.vector.memset(bias_rows[:, 1, :], 0.0)
        nc.scalar.dma_start(
            out=bias_rows[:, 0, :], in_=eb1.rearrange("t v e -> (t v e)").rearrange("(r c) -> r c", c=P)
        )
        nc.scalar.dma_start(
            out=bias_rows[0:COL_TILES, 1, :], in_=ebs1.rearrange("v e -> (v e)").rearrange("(r c) -> r c", c=P)
        )
        gate_pre = keep.tile([P, TASKS * ROW_TILES, GATES], BF16)
        nc.scalar.dma_start(out=gate_pre[:], in_=gate_pre1.rearrange("t (h p) g -> p (t h) g", p=P))
        gate_bias = keep.tile([P, TASKS, GATES], BF16)
        nc.scalar.dma_start(
            out=gate_bias[:].rearrange("p t g -> p (t g)"), in_=gb1.rearrange("t g -> (t g)").partition_broadcast(P)
        )

        x_rows = keep.tile([P, STREAMS, ROW_TILES, FEATURES], BF16)
        for s in NEED_ORDER:
            rows = share_h if s == SHARED else task_h[s]
            nc.sync.dma_start(out=x_rows[:, s, :, :], in_=rows.rearrange("(h p) u -> p h u", p=P))

        task_planes = keep.tile([P, COLS], U8, align_bytes=64)
        shared_planes = keep.tile([P, QUARTER], U8, align_bytes=64)
        nc.vector.memset(task_planes[:].bitcast(I32), 0)
        nc.vector.memset(shared_planes[:].bitcast(I32), 0)
        for quad in range(4):
            nc.sync.dma_start(
                out=task_planes[32 * quad : 32 * quad + 16, :].bitcast(I32),
                in_=ew1_scales[:, 4 * quad : 4 * quad + 4, :].bitcast(I32),
            )
        for quad in range(4):
            nc.sync.dma_start(
                out=shared_planes[32 * quad : 32 * quad + 16, :].bitcast(I32),
                in_=ews1_scales[0, 4 * quad : 4 * quad + 4, :].bitcast(I32).rearrange("r (k n) -> k r n", k=4),
            )

        words = keep.tile([P, STREAMS, COLS], U32, align_bytes=64)
        task_words = ew1_words.rearrange("t p n k -> t p (n k)").bitcast(I32)
        shared_words = ews1_words.rearrange("g p n k -> g p (n k)").bitcast(I32)
        for c in range(CHUNKS):
            cols = slice(c * CHUNK_COLS, (c + 1) * CHUNK_COLS)
            for s in NEED_ORDER:
                packed = shared_words[0] if s == SHARED else task_words[s]
                nc.sync.dma_start(out=words[:, s, cols].bitcast(I32), in_=packed[:, cols])

        by_expert = keep.tile([P, P], F32)
        nc.vector.tensor_copy(
            out=by_expert[:].rearrange("p (e v) -> p e v", e=EXPERTS),
            in_=identity[:].rearrange("p (v e) -> p e v", e=EXPERTS),
        )

        bias_rows_f = keep.tile([P, 2, P], F32)
        nc.vector.tensor_copy(out=bias_rows_f[:], in_=bias_rows[:])
        bias_t = z_pool.tile([P, 2, P], F32, tag="z")
        for plane in range(2):
            nc.tensor.transpose(out=bias_t[:, plane, :], in_=bias_rows_f[:, plane, :], identity=identity[:])
        bias_cols = keep.tile([P, 2, P], F32)
        nc.vector.tensor_copy(out=bias_cols[:], in_=bias_t[:])

        pairs = TASKS * ROW_TILES
        logits = keep.tile([P, pairs, GATES], F32)
        nc.vector.tensor_tensor(
            out=logits[:].rearrange("p (t h) g -> p t h g", h=ROW_TILES),
            in0=gate_pre[:].rearrange("p (t h) g -> p t h g", h=ROW_TILES),
            in1=gate_bias[:].unsqueeze(2).to_broadcast([P, TASKS, ROW_TILES, GATES]),
            op=ALU.add,
        )
        top = keep.tile([P, pairs], F32)
        nc.vector.tensor_reduce(out=top[:], in_=logits[:], axis=AX.X, op=ALU.max)
        shifted = keep.tile([P, pairs, GATES], F32)
        nc.vector.tensor_tensor(
            out=shifted[:], in0=logits[:], in1=top[:].unsqueeze(2).to_broadcast([P, pairs, GATES]), op=ALU.subtract
        )
        powers = keep.tile([P, pairs, GATES], F32)
        nc.scalar.activation(out=powers[:], in_=shifted[:], func=ACT.Exp)

        grouped = keep.tile([P, STREAMS, ROWS * 4], BF16, align_bytes=64)
        x_codes = keep.tile([P, STREAMS, ROWS], U32, align_bytes=64)
        x_planes = keep.tile([P, STREAMS, ROWS], U8, align_bytes=64)
        for turn, s in enumerate(NEED_ORDER):
            x_t = z_pool.tile([P, 2, ROWS], F32, tag="z")
            for h in range(ROW_TILES):
                x_words = x_rows[:, s, h, :].bitcast(F32)
                for half in range(2):
                    nc.tensor.transpose(
                        out=x_t[:, half, h * P : (h + 1) * P],
                        in_=x_words[:, half : FEATURES // 2 : 2],
                        identity=identity[:],
                    )
            side_by_side = grouped[:, s, :].bitcast(F32).rearrange("p (b half) -> p b half", half=2)
            if turn % 2 == 0:
                nc.vector.tensor_copy(out=side_by_side, in_=x_t[:].rearrange("p half b -> p b half"))
            else:
                nc.scalar.copy(out=side_by_side, in_=x_t[:].rearrange("p half b -> p b half"))
            for ready in [turn - 2] if turn < STREAMS - 1 else [turn - 2, turn - 1, turn]:
                if ready >= 0:
                    nc.vector.quantize_mx(
                        out=x_codes[:, NEED_ORDER[ready], :].bitcast(FP8X4),
                        scales=x_planes[:, NEED_ORDER[ready], :],
                        in_=grouped[:, NEED_ORDER[ready], :],
                    )

        total = keep.tile([P, pairs], F32)
        nc.vector.tensor_reduce(out=total[:], in_=powers[:], axis=AX.X, op=ALU.add)
        inverse = keep.tile([P, pairs], F32)
        nc.vector.reciprocal(out=inverse[:], in_=total[:])
        gate = keep.tile([P, pairs, GATES], F32)
        nc.vector.tensor_tensor(
            out=gate[:], in0=powers[:], in1=inverse[:].unsqueeze(2).to_broadcast([P, pairs, GATES]), op=ALU.mult
        )

        y_of_chunk = []

        def experts(run, vector_helps):
            c, place = divmod(run, STREAMS)
            s = NEED_ORDER[place]
            if place == 0:
                y_of_chunk.append(y_pool.tile([P, STREAMS, CHUNK_TILES, ROWS], F32, tag="y", name="y"))
            y = y_of_chunk[c]
            for first in range(0, CHUNK_TILES, 2):
                z = z_pool.tile([P, 2, ROWS], F32, tag="z")
                for i in range(2):
                    j = c * CHUNK_TILES + first + i
                    cols = slice(j * P, (j + 1) * P)
                    if s == SHARED:
                        k = j * P // QUARTER
                        plane = shared_planes[4 * k : P, j * P - k * QUARTER : (j + 1) * P - k * QUARTER]
                    else:
                        plane = task_planes[4 * s : P, cols]
                    nc.tensor.matmul_mx(
                        out=z[:, i, :],
                        lhsT=words[:, s, cols].bitcast(FP8X4),
                        lhsT_scale=plane,
                        rhs=x_codes[:, s, :].bitcast(FP8X4),
                        rhs_scale=x_planes[:, s, :],
                        start=True,
                        stop=True,
                    )
                for i in range(2):
                    j = c * CHUNK_TILES + first + i
                    bias = bias_cols[:, 1, j : j + 1] if s == SHARED else bias_cols[:, 0, 32 * s + j : 32 * s + j + 1]
                    if vector_helps and first > 0:
                        nc.vector.tensor_scalar(
                            out=y[:, s, first + i, :], in0=z[:, i, :], scalar1=bias, scalar2=0.0, op0=ALU.add, op1=ALU.max
                        )
                    else:
                        nc.scalar.activation(out=y[:, s, first + i, :], in_=z[:, i, :], func=ACT.Relu, bias=bias)

        def vector_starts(job):
            return job % VECTOR_STARTS == 0 and job < (CHUNKS - 1) * ROW_TILES * TASKS

        own_terms = {}
        shared_terms = {}
        sums = {}
        results = {}

        def bank(group, s):
            c, h = divmod(group, ROW_TILES)
            if s == SHARED:
                y_t = shared_pool.tile([P, EXPERTS, CHUNK_TILES, UNITS_PER_TILE], F32, tag="shared")
            else:
                y_t = own_pool.tile([P, EXPERTS, CHUNK_TILES, UNITS_PER_TILE], F32, tag="own")
            for i in range(CHUNK_TILES):
                nc.tensor.transpose(
                    out=y_t[:, :, i, :], in_=y_of_chunk[c][:, s, i, h * P : (h + 1) * P], identity=by_expert[:]
                )
            terms = y_t[:].rearrange("p e i v -> p e (i v)")
            if s == SHARED:
                shared_terms[group] = terms
            else:
                job = group * TASKS + s
                own_terms[job] = terms
                sums[job] = acc_pool.tile([P, PARTS, CHUNK_UNITS], F32, tag="acc", name="acc")
                if not vector_starts(job):
                    for part in range(PARTS):
                        nc.scalar.activation(
                            out=sums[job][:, part, :],
                            in_=terms[:, part, :],
                            func=ACT.Copy,
                            scale=gate[:, s * ROW_TILES + h, part : part + 1],
                        )
            number = group * STREAMS + NEED_ORDER.index(s)
            for run in runs_behind.get(number, []):
                experts(run, False)

        runs_behind = {}
        for run in range(4, RUNS):
            place = run - 4 if run < STREAMS else 2 * (run - STREAMS) + 1 + 2
            runs_behind.setdefault(place, []).append(run)

        for run in range(4):
            experts(run, True)
        for s in NEED_ORDER[: OWN_BANKS + 1]:
            bank(0, s)

        for r in range(STAGGER * (JOBS - 1) + JOB_ROUNDS):
            for job in range(JOBS):
                step = r - STAGGER * job
                if step < 0 or step >= JOB_ROUNDS:
                    continue
                group, t = divmod(job, TASKS)
                c, h = divmod(group, ROW_TILES)
                if step == 0:
                    if vector_starts(job):
                        nc.vector.tensor_tensor(
                            out=sums[job][:],
                            in0=own_terms[job][:, 0:PARTS, :],
                            in1=gate[:, t * ROW_TILES + h, 0:PARTS]
                            .unsqueeze(2)
                            .to_broadcast([P, PARTS, CHUNK_UNITS]),
                            op=ALU.mult,
                        )
                    continue
                for part in range(PARTS):
                    e = (PARTS * step + part) % EXPERTS
                    own = step < JOB_ROUNDS // 2
                    g = e if own else EXPERTS + e
                    nc.vector.scalar_tensor_tensor(
                        out=sums[job][:, part, :],
                        in0=own_terms[job][:, e, :] if own else shared_terms[group][:, e, :],
                        scalar=gate[:, t * ROW_TILES + h, g : g + 1],
                        in1=sums[job][:, part, :],
                        op0=ALU.mult,
                        op1=ALU.add,
                    )
                if step == JOB_ROUNDS - 1:
                    if t == 0:
                        results[group] = result_pool.tile([P, TASKS, CHUNK_UNITS], F32, tag="result", name="result")
                    joiner = nc.vector if job >= JOBS - 1 else nc.gpsimd
                    joiner.tensor_tensor(
                        out=sums[job][:, 0:2, :], in0=sums[job][:, 0:2, :], in1=sums[job][:, 2:4, :], op=ALU.add
                    )
                    joiner.tensor_tensor(
                        out=results[group][:, t, :],
                        in0=sums[job][:, 0, :],
                        in1=sums[job][:, 1, :],
                        op=ALU.add,
                    )
                    tasks = slice(t, t + 1) if group == GROUPS - 1 else slice(0, TASKS)
                    if t == TASKS - 1 or group == GROUPS - 1:
                        units = slice(c * CHUNK_UNITS, (c + 1) * CHUNK_UNITS)
                        nc.sync.dma_start(
                            out=out[tasks, h * P : (h + 1) * P, units].rearrange("t p v -> p t v"),
                            in_=results[group][:, tasks, :],
                        )
            done_with_own_bank, odd = divmod(r - (JOB_ROUNDS // 2 - 1), STAGGER)
            job = done_with_own_bank + OWN_BANKS
            if odd == 0 and done_with_own_bank >= 0 and job < JOBS:
                group, t = divmod(job, TASKS)
                if NEED_ORDER[NEED_ORDER.index(t) - 1] == SHARED:
                    bank(group, SHARED)
                bank(group, t)
